import numpy as np
import ml_dtypes


def mxq(x, axis, fmt="e4m3"):
    dtype, down = {"e4m3": (ml_dtypes.float8_e4m3fn, 7), "e5m2": (ml_dtypes.float8_e5m2, 14)}[fmt]
    v = np.moveaxis(np.asarray(x, np.float32).astype(ml_dtypes.bfloat16).astype(np.float64), axis, -1)
    blocks = v.reshape(v.shape[:-1] + (-1, 32))
    amax = np.abs(blocks).max(-1, keepdims=True)
    byte = np.maximum(np.where(amax > 0, np.frexp(amax)[1] - 1 + 127, 0) - down, 1)
    scale = np.exp2(byte - 127.0)
    codes = (blocks / scale).astype(np.float32).astype(dtype).astype(np.float64)
    return np.moveaxis((codes * scale).reshape(v.shape), -1, axis)


WIDE = False


def mx_kscale(k):
    if not WIDE:
        return np.ones(k)
    levels = np.array([10, -10, 5, -5, 0])
    a = np.random.permutation(np.resize(levels, k // 512 * 4)).reshape(k // 512, 4)
    idx = np.arange(k)
    return np.exp2(a[idx // 512, idx % 128 // 32])


BF16 = ml_dtypes.bfloat16


def bf(x):
    return np.asarray(x, np.float32).astype(BF16)


def f64(x):
    return np.asarray(x).astype(np.float64)


B, W, U, H, D, K, MAX_BACK, MAX_FWD = 2, 8, 256, 1, 1024, 512, 255, 0
CH = H * D
F = MAX_BACK + MAX_FWD + 1


def setup_inputs():
    s, t = mx_kscale(CH), mx_kscale(D)
    a = 1.5 * D ** -0.25
    return {"queries": bf(np.random.standard_normal((B, W, U, H, D)) * a * t),
            "keys": bf(np.random.standard_normal((B, W, K, H, D)) * a / t),
            "sin_emb": bf(np.random.standard_normal((F, CH)) * np.sqrt(0.5) * s),
            "pos_w": bf(np.random.standard_normal((CH, CH)) * 2.0 * D ** -0.25 / np.sqrt(CH) / s[None, :] / np.tile(t, H)[:, None])}


def relative_shift(x):
    pad = K + 1 - F
    x = np.pad(x, ((0, 0), (0, 0), (0, 0), (0, 0), (0, pad)))
    x = x.reshape(B, H, W, U * (K + 1))[:, :, :, : U * K]
    return x.reshape(B, H, W, U, K)


def reference(queries, keys, sin_emb, pos_w):
    proj = (mxq(f64(sin_emb), 1, "e4m3") @ mxq(f64(pos_w), 1, "e4m3").T).reshape(F, H, D)
    qq = mxq(f64(queries), 4, "e4m3").transpose(0, 3, 1, 2, 4)
    kq = mxq(f64(keys), 4, "e4m3").transpose(0, 3, 1, 4, 2)
    pq = mxq(proj, 2, "e4m3").transpose(1, 2, 0)[None, :, None]
    term_ac = qq @ kq
    term_bd = qq @ pq
    return term_ac + relative_shift(term_bd)

@@ -1,0 +1,204 @@
+from contextlib import ExitStack
+
+import concourse.mybir as mybir
+from concourse.masks import make_identity
+
+F32 = mybir.dt.float32
+BF16 = mybir.dt.bfloat16
+U32 = mybir.dt.uint32
+U8 = mybir.dt.uint8
+FP8X4 = mybir.dt.float8_e4m3fn_x4
+ADD = mybir.AluOpType.add
+IS_GE = mybir.AluOpType.is_ge
+
+P = 128
+NBLK = 16
+U = 256
+C = 512
+D = 1024
+F = 256
+LEAD = 3
+PITCH = 128 + 2 * F
+
+FLOPS = 2 * F * D * D + NBLK * 2 * U * D * (C + F)
+
+
+def tile_gemma3naudiorelativepositionembedding_pa_t_kernel(tc, queries, keys, sin_emb, pos_w, out):
+    nc = tc.nc
+    q_view = queries.rearrange("b w (p e) h d -> (b w) p (e h d)", e=2)
+    k_view = keys.rearrange("b w (p t) h d -> (b w) p (t h d)", t=4)
+    s_view = sin_emb.rearrange("(p e) i -> p (e i)", e=2)
+    w_view = pos_w.rearrange("(h p e) i -> h p (e i)", h=4, e=2)
+    o_view = out.rearrange("b h w (t p) c -> (b h w) p t c", t=2)
+    o_flat = out.rearrange("b h w u c -> (b h w) (u c)")
+
+    with ExitStack() as ctx:
+        const = ctx.enter_context(tc.tile_pool(name="const", bufs=1))
+        raws = ctx.enter_context(tc.tile_pool(name="raws", bufs=4))
+        work = ctx.enter_context(tc.tile_pool(name="work", bufs=2))
+        keep = ctx.enter_context(tc.tile_pool(name="keep", bufs=LEAD + 2))
+        psum = ctx.enter_context(tc.psum_pool(name="psum", bufs=2))
+
+        ident = const.tile([P, P], F32, name="ident")
+        make_identity(nc, ident[:])
+
+        lows = []
+        for n in range(LEAD + 2):
+            low = const.tile([P, 4, 128], F32, name="low%d" % n)
+            nc.gpsimd.memset(low[:], 0.0)
+            lows.append(low)
+
+        def copy_out(engine, dst, src):
+            if engine == 0:
+                nc.scalar.copy(out=dst, in_=src)
+            else:
+                nc.vector.tensor_copy(out=dst, in_=src)
+
+        def quantise_pair_rows(src, codes, scales, natural, engines):
+            raw = raws.tile([P, 2 * D], BF16, tag="qraw", bufs=5)
+            nc.sync.dma_start(out=raw[:], in_=src)
+            words = raw[:].bitcast(F32)
+            grouped = work.tile([P, 2 * U * 4], BF16, tag="qg", align_bytes=64)
+            g32 = grouped[:].bitcast(F32).rearrange("p (g c u) -> p g c u", g=2, u=2)
+            for g in range(2):
+                bank = psum.tile([P, 4, P], F32, tag="tp", bufs=4)
+                for e in range(2):
+                    for u2 in range(2):
+                        col = 512 * e + 128 * (2 * g + u2)
+                        nc.tensor.transpose(bank[:, 2 * e + u2, :], words[:, col : col + 128], ident[:])
+                if natural:
+                    dst = g32[:, g].rearrange("p (r e) u -> p r e u", e=2)
+                    bsrc = bank[:].rearrange("p (e u) r -> p r e u", e=2)
+                else:
+                    dst = g32[:, g].rearrange("p (e r) u -> p e r u", e=2)
+                    bsrc = bank[:].rearrange("p (e u) r -> p e r u", e=2)
+                copy_out(engines[g], dst, bsrc)
+            nc.vector.quantize_mx(out=codes.bitcast(FP8X4), scales=scales, in_=grouped[:])
+
+        s_codes = const.tile([P, 2 * F], U32, name="s_codes", align_bytes=64)
+        s_scales = const.tile([P, 2 * F], U8, name="s_scales", align_bytes=64)
+        quantise_pair_rows(s_view, s_codes[:], s_scales[:], True, (0, 1))
+        w_codes = const.tile([P, 4, 512], U32, name="w_codes", align_bytes=64)
+        w_scales = const.tile([P, 4, 512], U8, name="w_scales", align_bytes=64)
+        for h in range(4):
+            quantise_pair_rows(w_view[h], w_codes[:, h, :], w_scales[:, h, :], False, (0, 1))
+
+        p_grouped = const.tile([P, 2 * F * 4], BF16, name="p_grouped", align_bytes=64)
+        pg = p_grouped[:].rearrange("p (g f t) -> p g f t", g=2, t=4)
+        p_codes = const.tile([P, 2 * F], U32, name="p_codes", align_bytes=64)
+        p_scales = const.tile([P, 2 * F], U8, name="p_scales", align_bytes=64)
+        for g in range(2):
+            for fh in range(2):
+                pb = psum.tile([P, 4, 128], F32, tag="bd", bufs=2)
+                for t in range(4):
+                    h = 2 * g + t // 2
+                    e = t % 2
+                    for gi in range(2):
+                        wcol = 256 * gi + 128 * e
+                        scol = 256 * gi + 128 * fh
+                        nc.tensor.matmul_mx(
+                            out=pb[:, t, :],
+                            lhsT=w_codes[:, h, wcol : wcol + 128].bitcast(FP8X4),
+                            lhsT_scale=w_scales[:, h, wcol : wcol + 128],
+                            rhs=s_codes[:, scol : scol + 128].bitcast(FP8X4),
+                            rhs_scale=s_scales[:, scol : scol + 128],
+                            start=(gi == 0),
+                            stop=(gi == 1),
+                        )
+                copy_out(fh, pg[:, g, 128 * fh : 128 * fh + 128, :], pb[:].rearrange("p t f -> p f t"))
+        nc.vector.quantize_mx(out=p_codes[:].bitcast(FP8X4), scales=p_scales[:], in_=p_grouped[:])
+
+        q_state = {}
+
+        def query_stage(j):
+            q_codes = keep.tile([P, 2 * U], U32, tag="q_codes", align_bytes=64)
+            q_scales = keep.tile([P, 2 * U], U8, tag="q_scales", align_bytes=64)
+            quantise_pair_rows(q_view[j], q_codes[:], q_scales[:], True, (0, 0))
+            bd = psum.tile([P, 2, F], F32, tag="bd", bufs=2)
+            for t in range(2):
+                for g in range(2):
+                    qcol = 256 * g + 128 * t
+                    nc.tensor.matmul_mx(
+                        out=bd[:, t, :],
+                        lhsT=q_codes[:, qcol : qcol + 128].bitcast(FP8X4),
+                        lhsT_scale=q_scales[:, qcol : qcol + 128],
+                        rhs=p_codes[:, 256 * g : 256 * g + 256].bitcast(FP8X4),
+                        rhs_scale=p_scales[:, 256 * g : 256 * g + 256],
+                        start=(g == 0),
+                        stop=(g == 1),
+                    )
+            park = work.tile([P, PITCH], F32, tag="park", bufs=3)
+            nc.scalar.copy(out=park[:, 128:PITCH], in_=bd[:].rearrange("p t f -> p (t f)"))
+            nc.scalar.copy(out=park[:, 0:128], in_=bd[:, 1, 128:256])
+            nc.scalar.dma_start(
+                out=o_flat[j, 0 : P * PITCH].rearrange("(p s) -> p s", s=PITCH), in_=park[:]
+            )
+            x = keep.tile([P, 4, 128], F32, tag="x")
+            nc.sync.dma_start(
+                out=x[:].rearrange("p s j -> p (s j)"),
+                in_=o_flat[j, 128 : 128 + P * (PITCH - 1)].rearrange("(p s) -> p s", s=PITCH - 1)[:, 0:512],
+            )
+            low = lows[j % (LEAD + 2)]
+            for n in range(2):
+                shared = x[:, 2 * n, :]
+                nc.gpsimd.affine_select(
+                    out=low[:, 1 + n, :], in_=shared, pattern=[[-1, 128]],
+                    compare_op=IS_GE, fill=0.0, base=-1, channel_multiplier=1,
+                )
+                nc.gpsimd.affine_select(
+                    out=shared, in_=shared, pattern=[[1, 128]],
+                    compare_op=IS_GE, fill=0.0, base=0, channel_multiplier=-1,
+                )
+            q_state[j] = (q_codes, q_scales, x, low)
+
+        def key_stage(i):
+            q_codes, q_scales, x, low = q_state[i]
+            raw = raws.tile([P, 4 * D], BF16, tag="kraw", bufs=5)
+            nc.sync.dma_start(out=raw[:], in_=k_view[i])
+            words = raw[:].bitcast(F32)
+            grouped = work.tile([P, 2 * C * 4], BF16, tag="kg", align_bytes=64)
+            g32 = grouped[:].bitcast(F32).rearrange("p (g n u) -> p g n u", g=2, u=2)
+            for tt in range(4):
+                bank = psum.tile([P, 4, P], F32, tag="tp", bufs=4)
+                for w in range(4):
+                    col = 512 * tt + 128 * w
+                    nc.tensor.transpose(bank[:, w, :], words[:, col : col + 128], ident[:])
+                copy_out(
+                    1 if tt == 3 else 0,
+                    g32[:, :, 128 * tt : 128 * tt + 128, :],
+                    bank[:].rearrange("p (g u) r -> p g r u", g=2),
+                )
+            k_codes = work.tile([P, 2 * C], U32, tag="k_codes", align_bytes=64)
+            k_scales = work.tile([P, 2 * C], U8, tag="k_scales", align_bytes=64)
+            nc.vector.quantize_mx(out=k_codes[:].bitcast(FP8X4), scales=k_scales[:], in_=grouped[:])
+            res = work.tile([P, 2, C], F32, tag="res", bufs=3)
+            for t in range(2):
+                acc = psum.tile([P, C], F32, tag="ac", bufs=2)
+                for g in range(2):
+                    qcol = 256 * g + 128 * t
+                    nc.tensor.matmul_mx(
+                        out=acc[:],
+                        lhsT=q_codes[:, qcol : qcol + 128].bitcast(FP8X4),
+                        lhsT_scale=q_scales[:, qcol : qcol + 128],
+                        rhs=k_codes[:, 512 * g : 512 * g + 512].bitcast(FP8X4),
+                        rhs_scale=k_scales[:, 512 * g : 512 * g + 512],
+                        start=(g == 0),
+                        stop=(g == 1),
+                    )
+                a_seg = acc[:].rearrange("p (tt s r) -> p s r tt", tt=4, s=4)
+                o_seg = res[:, t, :].rearrange("p (s r tt) -> p s r tt", s=4, tt=4)
+                x_seg = x[:].rearrange("p s (r tt) -> p s r tt", tt=4)
+                l_seg = low[:].rearrange("p s (r tt) -> p s r tt", tt=4)
+                if t == 0:
+                    nc.vector.tensor_tensor(out=o_seg[:, 0:2], in0=a_seg[:, 0:2], in1=x_seg[:, 0:2], op=ADD)
+                    nc.vector.tensor_tensor(out=o_seg[:, 2:4], in0=a_seg[:, 2:4], in1=l_seg[:, 2:4], op=ADD)
+                else:
+                    nc.vector.tensor_tensor(out=o_seg[:, 1:3], in0=a_seg[:, 1:3], in1=x_seg[:, 2:4], op=ADD)
+                    nc.vector.tensor_tensor(out=o_seg[:, 0:4:3], in0=a_seg[:, 0:4:3], in1=l_seg[:, 0:2], op=ADD)
+            nc.sync.dma_start(out=o_view[i], in_=res[:])
+
+        for step in range(NBLK + LEAD):
+            if step < NBLK:
+                query_stage(step)
+            if step >= LEAD:
+                key_stage(step - LEAD)

@@ -17,8 +17,10 @@ U = 256
 C = 512
 D = 1024
 F = 256
-LEAD = 3
 PITCH = 128 + 2 * F
+STORE_LAG = 3
+AHEAD = 3
+NSTEP = NBLK + 4
 
 FLOPS = 2 * F * D * D + NBLK * 2 * U * D * (C + F)
 
@@ -34,16 +36,43 @@ def tile_gemma3naudiorelativepositionembedding_pa_t_kernel(tc, queries, keys, si
 
     with ExitStack() as ctx:
         const = ctx.enter_context(tc.tile_pool(name="const", bufs=1))
-        raws = ctx.enter_context(tc.tile_pool(name="raws", bufs=4))
+        raws = ctx.enter_context(tc.tile_pool(name="raws", bufs=6))
         work = ctx.enter_context(tc.tile_pool(name="work", bufs=2))
-        keep = ctx.enter_context(tc.tile_pool(name="keep", bufs=LEAD + 2))
+        keep = ctx.enter_context(tc.tile_pool(name="keep", bufs=5))
         psum = ctx.enter_context(tc.psum_pool(name="psum", bufs=2))
+        ctx.enter_context(tc.manual_schedule())
+
+        pair_raw = {}
+        k_raw = {}
+        pair_grouped = {}
+        q_mx = {}
+        k_grouped = {}
+        k_mx = {}
+        accs = {}
+        shifted = {}
+        results = {}
+
+        def load_pair_rows(key, src):
+            raw = raws.tile([P, 2 * D], BF16, tag="qraw", bufs=8)
+            nc.sync.dma_start(out=raw[:], in_=src)
+            pair_raw[key] = raw
+
+        def load_k(i):
+            raw = raws.tile([P, 4 * D], BF16, tag="kraw", bufs=8)
+            nc.sync.dma_start(out=raw[:], in_=k_view[i])
+            k_raw[i] = raw
+
+        load_pair_rows("s", s_view)
+        for h in range(4):
+            load_pair_rows("w%d" % h, w_view[h])
+        for n in range(AHEAD):
+            load_pair_rows(n, q_view[n])
+            load_k(n)
 
         ident = const.tile([P, P], F32, name="ident")
         make_identity(nc, ident[:])
-
         lows = []
-        for n in range(LEAD + 2):
+        for n in range(4):
             low = const.tile([P, 4, 128], F32, name="low%d" % n)
             nc.gpsimd.memset(low[:], 0.0)
             lows.append(low)
@@ -54,11 +83,9 @@ def tile_gemma3naudiorelativepositionembedding_pa_t_kernel(tc, queries, keys, si
             else:
                 nc.vector.tensor_copy(out=dst, in_=src)
 
-        def quantise_pair_rows(src, codes, scales, natural, engines):
-            raw = raws.tile([P, 2 * D], BF16, tag="qraw", bufs=5)
-            nc.sync.dma_start(out=raw[:], in_=src)
-            words = raw[:].bitcast(F32)
-            grouped = work.tile([P, 2 * U * 4], BF16, tag="qg", align_bytes=64)
+        def transpose_pair_rows(key, natural, engines):
+            words = pair_raw[key][:].bitcast(F32)
+            grouped = work.tile([P, 2 * U * 4], BF16, tag="qg", bufs=3, align_bytes=64)
             g32 = grouped[:].bitcast(F32).rearrange("p (g c u) -> p g c u", g=2, u=2)
             for g in range(2):
                 bank = psum.tile([P, 4, P], F32, tag="tp", bufs=4)
@@ -73,47 +100,58 @@ def tile_gemma3naudiorelativepositionembedding_pa_t_kernel(tc, queries, keys, si
                     dst = g32[:, g].rearrange("p (e r) u -> p e r u", e=2)
                     bsrc = bank[:].rearrange("p (e u) r -> p e r u", e=2)
                 copy_out(engines[g], dst, bsrc)
-            nc.vector.quantize_mx(out=codes.bitcast(FP8X4), scales=scales, in_=grouped[:])
+            pair_grouped[key] = grouped
+
+        def quantise_pair_rows(key, codes, scales):
+            nc.vector.quantize_mx(out=codes.bitcast(FP8X4), scales=scales, in_=pair_grouped[key][:])
 
         s_codes = const.tile([P, 2 * F], U32, name="s_codes", align_bytes=64)
         s_scales = const.tile([P, 2 * F], U8, name="s_scales", align_bytes=64)
-        quantise_pair_rows(s_view, s_codes[:], s_scales[:], True, (0, 1))
         w_codes = const.tile([P, 4, 512], U32, name="w_codes", align_bytes=64)
         w_scales = const.tile([P, 4, 512], U8, name="w_scales", align_bytes=64)
-        for h in range(4):
-            quantise_pair_rows(w_view[h], w_codes[:, h, :], w_scales[:, h, :], False, (0, 1))
-
         p_grouped = const.tile([P, 2 * F * 4], BF16, name="p_grouped", align_bytes=64)
         pg = p_grouped[:].rearrange("p (g f t) -> p g f t", g=2, t=4)
         p_codes = const.tile([P, 2 * F], U32, name="p_codes", align_bytes=64)
         p_scales = const.tile([P, 2 * F], U8, name="p_scales", align_bytes=64)
-        for g in range(2):
-            for fh in range(2):
-                pb = psum.tile([P, 4, 128], F32, tag="bd", bufs=2)
-                for t in range(4):
-                    h = 2 * g + t // 2
-                    e = t % 2
-                    for gi in range(2):
-                        wcol = 256 * gi + 128 * e
-                        scol = 256 * gi + 128 * fh
-                        nc.tensor.matmul_mx(
-                            out=pb[:, t, :],
-                            lhsT=w_codes[:, h, wcol : wcol + 128].bitcast(FP8X4),
-                            lhsT_scale=w_scales[:, h, wcol : wcol + 128],
-                            rhs=s_codes[:, scol : scol + 128].bitcast(FP8X4),
-                            rhs_scale=s_scales[:, scol : scol + 128],
-                            start=(gi == 0),
-                            stop=(gi == 1),
-                        )
-                copy_out(fh, pg[:, g, 128 * fh : 128 * fh + 128, :], pb[:].rearrange("p t f -> p f t"))
-        nc.vector.quantize_mx(out=p_codes[:].bitcast(FP8X4), scales=p_scales[:], in_=p_grouped[:])
 
-        q_state = {}
+        transpose_pair_rows("s", True, (0, 1))
+        transpose_pair_rows("w0", False, (0, 1))
+        quantise_pair_rows("s", s_codes[:], s_scales[:])
+        for h in range(1, 4):
+            transpose_pair_rows("w%d" % h, False, (0, 1))
+            quantise_pair_rows("w%d" % (h - 1), w_codes[:, h - 1, :], w_scales[:, h - 1, :])
 
-        def query_stage(j):
+        def project():
+            quantise_pair_rows("w3", w_codes[:, 3, :], w_scales[:, 3, :])
+            for g in range(2):
+                for fh in range(2):
+                    pb = psum.tile([P, 4, 128], F32, tag="bd", bufs=2)
+                    for t in range(4):
+                        h = 2 * g + t // 2
+                        e = t % 2
+                        for gi in range(2):
+                            wcol = 256 * gi + 128 * e
+                            scol = 256 * gi + 128 * fh
+                            nc.tensor.matmul_mx(
+                                out=pb[:, t, :],
+                                lhsT=w_codes[:, h, wcol : wcol + 128].bitcast(FP8X4),
+                                lhsT_scale=w_scales[:, h, wcol : wcol + 128],
+                                rhs=s_codes[:, scol : scol + 128].bitcast(FP8X4),
+                                rhs_scale=s_scales[:, scol : scol + 128],
+                                start=(gi == 0),
+                                stop=(gi == 1),
+                            )
+                    copy_out(fh, pg[:, g, 128 * fh : 128 * fh + 128, :], pb[:].rearrange("p t f -> p f t"))
+            nc.vector.quantize_mx(out=p_codes[:].bitcast(FP8X4), scales=p_scales[:], in_=p_grouped[:])
+
+        def quantise_q(j):
             q_codes = keep.tile([P, 2 * U], U32, tag="q_codes", align_bytes=64)
             q_scales = keep.tile([P, 2 * U], U8, tag="q_scales", align_bytes=64)
-            quantise_pair_rows(q_view[j], q_codes[:], q_scales[:], True, (0, 0))
+            quantise_pair_rows(j, q_codes[:], q_scales[:])
+            q_mx[j] = (q_codes, q_scales)
+
+        def positions(j):
+            q_codes, q_scales = q_mx[j]
             bd = psum.tile([P, 2, F], F32, tag="bd", bufs=2)
             for t in range(2):
                 for g in range(2):
@@ -130,15 +168,17 @@ def tile_gemma3naudiorelativepositionembedding_pa_t_kernel(tc, queries, keys, si
             park = work.tile([P, PITCH], F32, tag="park", bufs=3)
             nc.scalar.copy(out=park[:, 128:PITCH], in_=bd[:].rearrange("p t f -> p (t f)"))
             nc.scalar.copy(out=park[:, 0:128], in_=bd[:, 1, 128:256])
-            nc.scalar.dma_start(
+            nc.sync.dma_start(
                 out=o_flat[j, 0 : P * PITCH].rearrange("(p s) -> p s", s=PITCH), in_=park[:]
             )
-            x = keep.tile([P, 4, 128], F32, tag="x")
+
+        def read_back(j):
+            x = keep.tile([P, 4, 128], F32, tag="x", bufs=4)
             nc.sync.dma_start(
                 out=x[:].rearrange("p s j -> p (s j)"),
                 in_=o_flat[j, 128 : 128 + P * (PITCH - 1)].rearrange("(p s) -> p s", s=PITCH - 1)[:, 0:512],
             )
-            low = lows[j % (LEAD + 2)]
+            low = lows[j % 4]
             for n in range(2):
                 shared = x[:, 2 * n, :]
                 nc.gpsimd.affine_select(
@@ -149,16 +189,15 @@ def tile_gemma3naudiorelativepositionembedding_pa_t_kernel(tc, queries, keys, si
                     out=shared, in_=shared, pattern=[[1, 128]],
                     compare_op=IS_GE, fill=0.0, base=0, channel_multiplier=-1,
                 )
-            q_state[j] = (q_codes, q_scales, x, low)
+            shifted[j] = (x, low)
 
-        def key_stage(i):
-            q_codes, q_scales, x, low = q_state[i]
-            raw = raws.tile([P, 4 * D], BF16, tag="kraw", bufs=5)
-            nc.sync.dma_start(out=raw[:], in_=k_view[i])
-            words = raw[:].bitcast(F32)
-            grouped = work.tile([P, 2 * C * 4], BF16, tag="kg", align_bytes=64)
+        def transpose_k(i, half):
+            words = k_raw[i][:].bitcast(F32)
+            if half == 0:
+                k_grouped[i] = work.tile([P, 2 * C * 4], BF16, tag="kg", align_bytes=64, name="kg")
+            grouped = k_grouped[i]
             g32 = grouped[:].bitcast(F32).rearrange("p (g n u) -> p g n u", g=2, u=2)
-            for tt in range(4):
+            for tt in range(2 * half, 2 * half + 2):
                 bank = psum.tile([P, 4, P], F32, tag="tp", bufs=4)
                 for w in range(4):
                     col = 512 * tt + 128 * w
@@ -168,37 +207,82 @@ def tile_gemma3naudiorelativepositionembedding_pa_t_kernel(tc, queries, keys, si
                     g32[:, :, 128 * tt : 128 * tt + 128, :],
                     bank[:].rearrange("p (g u) r -> p g r u", g=2),
                 )
+
+        def quantise_k(i):
             k_codes = work.tile([P, 2 * C], U32, tag="k_codes", align_bytes=64)
             k_scales = work.tile([P, 2 * C], U8, tag="k_scales", align_bytes=64)
-            nc.vector.quantize_mx(out=k_codes[:].bitcast(FP8X4), scales=k_scales[:], in_=grouped[:])
-            res = work.tile([P, 2, C], F32, tag="res", bufs=3)
-            for t in range(2):
-                acc = psum.tile([P, C], F32, tag="ac", bufs=2)
-                for g in range(2):
-                    qcol = 256 * g + 128 * t
-                    nc.tensor.matmul_mx(
-                        out=acc[:],
-                        lhsT=q_codes[:, qcol : qcol + 128].bitcast(FP8X4),
-                        lhsT_scale=q_scales[:, qcol : qcol + 128],
-                        rhs=k_codes[:, 512 * g : 512 * g + 512].bitcast(FP8X4),
-                        rhs_scale=k_scales[:, 512 * g : 512 * g + 512],
-                        start=(g == 0),
-                        stop=(g == 1),
-                    )
-                a_seg = acc[:].rearrange("p (tt s r) -> p s r tt", tt=4, s=4)
-                o_seg = res[:, t, :].rearrange("p (s r tt) -> p s r tt", s=4, tt=4)
-                x_seg = x[:].rearrange("p s (r tt) -> p s r tt", tt=4)
-                l_seg = low[:].rearrange("p s (r tt) -> p s r tt", tt=4)
-                if t == 0:
-                    nc.vector.tensor_tensor(out=o_seg[:, 0:2], in0=a_seg[:, 0:2], in1=x_seg[:, 0:2], op=ADD)
-                    nc.vector.tensor_tensor(out=o_seg[:, 2:4], in0=a_seg[:, 2:4], in1=l_seg[:, 2:4], op=ADD)
-                else:
-                    nc.vector.tensor_tensor(out=o_seg[:, 1:3], in0=a_seg[:, 1:3], in1=x_seg[:, 2:4], op=ADD)
-                    nc.vector.tensor_tensor(out=o_seg[:, 0:4:3], in0=a_seg[:, 0:4:3], in1=l_seg[:, 0:2], op=ADD)
-            nc.sync.dma_start(out=o_view[i], in_=res[:])
+            nc.vector.quantize_mx(out=k_codes[:].bitcast(FP8X4), scales=k_scales[:], in_=k_grouped[i][:])
+            k_mx[i] = (k_codes, k_scales)
 
-        for step in range(NBLK + LEAD):
-            if step < NBLK:
-                query_stage(step)
-            if step >= LEAD:
-                key_stage(step - LEAD)
+        def content(i, t):
+            q_codes, q_scales = q_mx[i]
+            k_codes, k_scales = k_mx[i]
+            acc = psum.tile([P, C], F32, tag="ac", bufs=2)
+            for g in range(2):
+                qcol = 256 * g + 128 * t
+                nc.tensor.matmul_mx(
+                    out=acc[:],
+                    lhsT=q_codes[:, qcol : qcol + 128].bitcast(FP8X4),
+                    lhsT_scale=q_scales[:, qcol : qcol + 128],
+                    rhs=k_codes[:, 512 * g : 512 * g + 512].bitcast(FP8X4),
+                    rhs_scale=k_scales[:, 512 * g : 512 * g + 512],
+                    start=(g == 0),
+                    stop=(g == 1),
+                )
+            accs[(i, t)] = acc
+
+        def add_up(i, t):
+            if t == 0:
+                results[i] = work.tile([P, 2, C], F32, tag="res", bufs=STORE_LAG + 2, name="res")
+            res = results[i]
+            x, low = shifted[i]
+            a_seg = accs[(i, t)][:].rearrange("p (tt s r) -> p s r tt", tt=4, s=4)
+            o_seg = res[:, t, :].rearrange("p (s r tt) -> p s r tt", s=4, tt=4)
+            x_seg = x[:].rearrange("p s (r tt) -> p s r tt", tt=4)
+            l_seg = low[:].rearrange("p s (r tt) -> p s r tt", tt=4)
+            if t == 0:
+                nc.vector.tensor_tensor(out=o_seg[:, 0:2], in0=a_seg[:, 0:2], in1=x_seg[:, 0:2], op=ADD)
+                nc.vector.tensor_tensor(out=o_seg[:, 2:4], in0=a_seg[:, 2:4], in1=l_seg[:, 2:4], op=ADD)
+            else:
+                nc.vector.tensor_tensor(out=o_seg[:, 1:3], in0=a_seg[:, 1:3], in1=x_seg[:, 2:4], op=ADD)
+                nc.vector.tensor_tensor(out=o_seg[:, 0:4:3], in0=a_seg[:, 0:4:3], in1=l_seg[:, 0:2], op=ADD)
+
+        stored = [0]
+
+        def store_up_to(last, queue):
+            while stored[0] <= last:
+                queue.dma_start(out=o_view[stored[0]], in_=results[stored[0]][:])
+                stored[0] += 1
+
+        for s in range(NSTEP):
+            j_t, j_b, j_r, i_t, i_a = s, s - 1, s - 2, s - 3, s - 4
+            has_k = 0 <= i_t < NBLK
+            has_a = 0 <= i_a
+            has_b = 0 <= j_b < NBLK
+            if s + AHEAD < NBLK:
+                load_pair_rows(s + AHEAD, q_view[s + AHEAD])
+                load_k(s + AHEAD)
+            store_up_to(i_a - (STORE_LAG if s < NSTEP - 2 else 1), nc.sync)
+            if 0 <= j_r < NBLK:
+                read_back(j_r)
+            if has_b:
+                quantise_q(j_b)
+            if has_k:
+                transpose_k(i_t, 0)
+            if has_a:
+                content(i_a, 0)
+                add_up(i_a, 0)
+            if has_k:
+                transpose_k(i_t, 1)
+            if has_a:
+                content(i_a, 1)
+                add_up(i_a, 1)
+            if j_t < NBLK:
+                transpose_pair_rows(j_t, True, (0, 0))
+            if s == 0:
+                project()
+            if has_b:
+                positions(j_b)
+            if has_k:
+                quantise_k(i_t)
+        store_up_to(NBLK - 1, nc.sync)

@@ -18,9 +18,12 @@ C = 512
 D = 1024
 F = 256
 PITCH = 128 + 2 * F
-STORE_LAG = 3
-AHEAD = 3
-NSTEP = NBLK + 4
+Q_AHEAD = 8
+B_AHEAD = 4
+K_LOAD = 2
+Q_LOAD = Q_AHEAD + 2
+STORE_LAG = 7
+EARLY_K_LOADS = {-6: 0, -5: 1, -3: 2, -1: 3}
 
 FLOPS = 2 * F * D * D + NBLK * 2 * U * D * (C + F)
 
@@ -38,7 +41,7 @@ def tile_gemma3naudiorelativepositionembedding_pa_t_kernel(tc, queries, keys, si
         const = ctx.enter_context(tc.tile_pool(name="const", bufs=1))
         raws = ctx.enter_context(tc.tile_pool(name="raws", bufs=6))
         work = ctx.enter_context(tc.tile_pool(name="work", bufs=2))
-        keep = ctx.enter_context(tc.tile_pool(name="keep", bufs=5))
+        keep = ctx.enter_context(tc.tile_pool(name="keep", bufs=Q_AHEAD + 3))
         psum = ctx.enter_context(tc.psum_pool(name="psum", bufs=2))
         ctx.enter_context(tc.manual_schedule())
 
@@ -58,21 +61,20 @@ def tile_gemma3naudiorelativepositionembedding_pa_t_kernel(tc, queries, keys, si
             pair_raw[key] = raw
 
         def load_k(i):
-            raw = raws.tile([P, 4 * D], BF16, tag="kraw", bufs=8)
+            raw = raws.tile([P, 4 * D], BF16, tag="kraw", bufs=4)
             nc.sync.dma_start(out=raw[:], in_=k_view[i])
             k_raw[i] = raw
 
         load_pair_rows("s", s_view)
         for h in range(4):
             load_pair_rows("w%d" % h, w_view[h])
-        for n in range(AHEAD):
+        for n in range(2):
             load_pair_rows(n, q_view[n])
-            load_k(n)
 
         ident = const.tile([P, P], F32, name="ident")
         make_identity(nc, ident[:])
         lows = []
-        for n in range(4):
+        for n in range(B_AHEAD + 2):
             low = const.tile([P, 4, 128], F32, name="low%d" % n)
             nc.gpsimd.memset(low[:], 0.0)
             lows.append(low)
@@ -173,12 +175,12 @@ def tile_gemma3naudiorelativepositionembedding_pa_t_kernel(tc, queries, keys, si
             )
 
         def read_back(j):
-            x = keep.tile([P, 4, 128], F32, tag="x", bufs=4)
+            x = keep.tile([P, 4, 128], F32, tag="x", bufs=B_AHEAD + 2)
             nc.sync.dma_start(
                 out=x[:].rearrange("p s j -> p (s j)"),
                 in_=o_flat[j, 128 : 128 + P * (PITCH - 1)].rearrange("(p s) -> p s", s=PITCH - 1)[:, 0:512],
             )
-            low = lows[j % 4]
+            low = lows[j % (B_AHEAD + 2)]
             for n in range(2):
                 shared = x[:, 2 * n, :]
                 nc.gpsimd.affine_select(
@@ -254,35 +256,36 @@ def tile_gemma3naudiorelativepositionembedding_pa_t_kernel(tc, queries, keys, si
                 queue.dma_start(out=o_view[stored[0]], in_=results[stored[0]][:])
                 stored[0] += 1
 
-        for s in range(NSTEP):
-            j_t, j_b, j_r, i_t, i_a = s, s - 1, s - 2, s - 3, s - 4
-            has_k = 0 <= i_t < NBLK
+        for s in range(-Q_AHEAD, NBLK + 1):
+            j_t, j_b, j_r, i_a = s + Q_AHEAD, s + B_AHEAD, s + B_AHEAD - 1, s - 1
+            has_k = 0 <= s < NBLK
             has_a = 0 <= i_a
-            has_b = 0 <= j_b < NBLK
-            if s + AHEAD < NBLK:
-                load_pair_rows(s + AHEAD, q_view[s + AHEAD])
-                load_k(s + AHEAD)
-            store_up_to(i_a - (STORE_LAG if s < NSTEP - 2 else 1), nc.sync)
+            if s in EARLY_K_LOADS:
+                load_k(EARLY_K_LOADS[s])
+            elif 4 <= s + K_LOAD < NBLK:
+                load_k(s + K_LOAD)
+            if 2 <= s + Q_LOAD < NBLK:
+                load_pair_rows(s + Q_LOAD, q_view[s + Q_LOAD])
+            store_up_to(i_a - STORE_LAG if s + K_LOAD < NBLK else i_a - 1, nc.sync)
             if 0 <= j_r < NBLK:
                 read_back(j_r)
-            if has_b:
-                quantise_q(j_b)
+            if 0 <= j_t - 1 < NBLK:
+                quantise_q(j_t - 1)
             if has_k:
-                transpose_k(i_t, 0)
+                transpose_k(s, 0)
             if has_a:
                 content(i_a, 0)
-                add_up(i_a, 0)
-            if has_k:
-                transpose_k(i_t, 1)
-            if has_a:
                 content(i_a, 1)
+                add_up(i_a, 0)
                 add_up(i_a, 1)
+            if has_k:
+                transpose_k(s, 1)
+            if 0 <= j_b < NBLK:
+                positions(j_b)
             if j_t < NBLK:
                 transpose_pair_rows(j_t, True, (0, 0))
-            if s == 0:
+            if s == -Q_AHEAD:
                 project()
-            if has_b:
-                positions(j_b)
             if has_k:
-                quantise_k(i_t)
+                quantise_k(s)
         store_up_to(NBLK - 1, nc.sync)

@@ -52,6 +52,7 @@ def tile_gemma3naudiorelativepositionembedding_pa_t_kernel(tc, queries, keys, si
         k_grouped = {}
         k_mx = {}
         accs = {}
+        bds = {}
         shifted = {}
         results = {}
 
@@ -152,21 +153,25 @@ def tile_gemma3naudiorelativepositionembedding_pa_t_kernel(tc, queries, keys, si
             quantise_pair_rows(j, q_codes[:], q_scales[:])
             q_mx[j] = (q_codes, q_scales)
 
-        def positions(j):
+        def positions(j, t):
             q_codes, q_scales = q_mx[j]
-            bd = psum.tile([P, 2, F], F32, tag="bd", bufs=2)
-            for t in range(2):
-                for g in range(2):
-                    qcol = 256 * g + 128 * t
-                    nc.tensor.matmul_mx(
-                        out=bd[:, t, :],
-                        lhsT=q_codes[:, qcol : qcol + 128].bitcast(FP8X4),
-                        lhsT_scale=q_scales[:, qcol : qcol + 128],
-                        rhs=p_codes[:, 256 * g : 256 * g + 256].bitcast(FP8X4),
-                        rhs_scale=p_scales[:, 256 * g : 256 * g + 256],
-                        start=(g == 0),
-                        stop=(g == 1),
-                    )
+            if t == 0:
+                bds[j] = psum.tile([P, 2, F], F32, tag="bd", bufs=2, name="bd")
+            bd = bds[j]
+            for g in range(2):
+                qcol = 256 * g + 128 * t
+                nc.tensor.matmul_mx(
+                    out=bd[:, t, :],
+                    lhsT=q_codes[:, qcol : qcol + 128].bitcast(FP8X4),
+                    lhsT_scale=q_scales[:, qcol : qcol + 128],
+                    rhs=p_codes[:, 256 * g : 256 * g + 256].bitcast(FP8X4),
+                    rhs_scale=p_scales[:, 256 * g : 256 * g + 256],
+                    start=(g == 0),
+                    stop=(g == 1),
+                )
+
+        def park_rows(j):
+            bd = bds[j]
             park = work.tile([P, PITCH], F32, tag="park", bufs=3)
             nc.scalar.copy(out=park[:, 128:PITCH], in_=bd[:].rearrange("p t f -> p (t f)"))
             nc.scalar.copy(out=park[:, 0:128], in_=bd[:, 1, 128:256])
@@ -193,13 +198,13 @@ def tile_gemma3naudiorelativepositionembedding_pa_t_kernel(tc, queries, keys, si
                 )
             shifted[j] = (x, low)
 
-        def transpose_k(i, half):
+        def transpose_k(i, banks):
             words = k_raw[i][:].bitcast(F32)
-            if half == 0:
+            if banks[0] == 0:
                 k_grouped[i] = work.tile([P, 2 * C * 4], BF16, tag="kg", align_bytes=64, name="kg")
             grouped = k_grouped[i]
             g32 = grouped[:].bitcast(F32).rearrange("p (g n u) -> p g n u", g=2, u=2)
-            for tt in range(2 * half, 2 * half + 2):
+            for tt in banks:
                 bank = psum.tile([P, 4, P], F32, tag="tp", bufs=4)
                 for w in range(4):
                     col = 512 * tt + 128 * w
@@ -220,7 +225,9 @@ def tile_gemma3naudiorelativepositionembedding_pa_t_kernel(tc, queries, keys, si
             q_codes, q_scales = q_mx[i]
             k_codes, k_scales = k_mx[i]
             acc = psum.tile([P, C], F32, tag="ac", bufs=2)
-            for g in range(2):
+            for g in (-1, 0, 1):
+                lone = g < 0
+                g = max(g, 0)
                 qcol = 256 * g + 128 * t
                 nc.tensor.matmul_mx(
                     out=acc[:],
@@ -229,7 +236,7 @@ def tile_gemma3naudiorelativepositionembedding_pa_t_kernel(tc, queries, keys, si
                     rhs=k_codes[:, 512 * g : 512 * g + 512].bitcast(FP8X4),
                     rhs_scale=k_scales[:, 512 * g : 512 * g + 512],
                     start=(g == 0),
-                    stop=(g == 1),
+                    stop=(g == 1 or lone),
                 )
             accs[(i, t)] = acc
 
@@ -271,21 +278,28 @@ def tile_gemma3naudiorelativepositionembedding_pa_t_kernel(tc, queries, keys, si
                 read_back(j_r)
             if 0 <= j_t - 1 < NBLK:
                 quantise_q(j_t - 1)
+            has_b = 0 <= j_b < NBLK
             if has_k:
-                transpose_k(s, 0)
+                transpose_k(s, (0, 1, 2))
             if has_a:
                 content(i_a, 0)
-                content(i_a, 1)
+            if has_b:
+                positions(j_b, 0)
+            if has_a:
                 add_up(i_a, 0)
-                add_up(i_a, 1)
             if has_k:
-                transpose_k(s, 1)
-            if 0 <= j_b < NBLK:
-                positions(j_b)
+                transpose_k(s, (3,))
             if j_t < NBLK:
                 transpose_pair_rows(j_t, True, (0, 0))
             if s == -Q_AHEAD:
                 project()
             if has_k:
                 quantise_k(s)
+            if has_a:
+                content(i_a, 1)
+            if has_b:
+                positions(j_b, 1)
+                park_rows(j_b)
+            if has_a:
+                add_up(i_a, 1)
         store_up_to(NBLK - 1, nc.sync)

@@ -53,6 +53,7 @@ def tile_gemma3naudiorelativepositionembedding_pa_t_kernel(tc, queries, keys, si
         k_mx = {}
         accs = {}
         bds = {}
+        parks = {}
         shifted = {}
         results = {}
 
@@ -175,8 +176,11 @@ def tile_gemma3naudiorelativepositionembedding_pa_t_kernel(tc, queries, keys, si
             park = work.tile([P, PITCH], F32, tag="park", bufs=3)
             nc.scalar.copy(out=park[:, 128:PITCH], in_=bd[:].rearrange("p t f -> p (t f)"))
             nc.scalar.copy(out=park[:, 0:128], in_=bd[:, 1, 128:256])
+            parks[j] = park
+
+        def park_write(j):
             nc.sync.dma_start(
-                out=o_flat[j, 0 : P * PITCH].rearrange("(p s) -> p s", s=PITCH), in_=park[:]
+                out=o_flat[j, 0 : P * PITCH].rearrange("(p s) -> p s", s=PITCH), in_=parks[j][:]
             )
 
         def read_back(j):
@@ -264,7 +268,7 @@ def tile_gemma3naudiorelativepositionembedding_pa_t_kernel(tc, queries, keys, si
                 stored[0] += 1
 
         for s in range(-Q_AHEAD, NBLK + 1):
-            j_t, j_b, j_r, i_a = s + Q_AHEAD, s + B_AHEAD, s + B_AHEAD - 1, s - 1
+            j_t, j_b, j_w, j_r, i_a = s + Q_AHEAD, s + B_AHEAD, s + B_AHEAD - 1, s + B_AHEAD - 2, s - 1
             has_k = 0 <= s < NBLK
             has_a = 0 <= i_a
             if s in EARLY_K_LOADS:
@@ -274,6 +278,8 @@ def tile_gemma3naudiorelativepositionembedding_pa_t_kernel(tc, queries, keys, si
             if 2 <= s + Q_LOAD < NBLK:
                 load_pair_rows(s + Q_LOAD, q_view[s + Q_LOAD])
             store_up_to(i_a - STORE_LAG if s + K_LOAD < NBLK else i_a - 1, nc.sync)
+            if 0 <= j_w < NBLK:
+                park_write(j_w)
             if 0 <= j_r < NBLK:
                 read_back(j_r)
             if 0 <= j_t - 1 < NBLK:

@@ -17,9 +17,9 @@ U = 256
 C = 512
 D = 1024
 F = 256
-PITCH = 128 + 2 * F
+PITCH = 128 + 4 * F
 Q_AHEAD = 8
-B_AHEAD = 4
+B_AHEAD = 6
 K_LOAD = 2
 Q_LOAD = Q_AHEAD + 2
 STORE_LAG = 7
@@ -35,7 +35,7 @@ def tile_gemma3naudiorelativepositionembedding_pa_t_kernel(tc, queries, keys, si
     s_view = sin_emb.rearrange("(p e) i -> p (e i)", e=2)
     w_view = pos_w.rearrange("(h p e) i -> h p (e i)", h=4, e=2)
     o_view = out.rearrange("b h w (t p) c -> (b h w) p t c", t=2)
-    o_flat = out.rearrange("b h w u c -> (b h w) (u c)")
+    o_flat = out.rearrange("b h (m w) u c -> (b h m) (w u c)", w=2)
 
     with ExitStack() as ctx:
         const = ctx.enter_context(tc.tile_pool(name="const", bufs=1))
@@ -76,7 +76,7 @@ def tile_gemma3naudiorelativepositionembedding_pa_t_kernel(tc, queries, keys, si
         ident = const.tile([P, P], F32, name="ident")
         make_identity(nc, ident[:])
         lows = []
-        for n in range(B_AHEAD + 2):
+        for n in range(6):
             low = const.tile([P, 4, 128], F32, name="low%d" % n)
             nc.gpsimd.memset(low[:], 0.0)
             lows.append(low)
@@ -173,34 +173,38 @@ def tile_gemma3naudiorelativepositionembedding_pa_t_kernel(tc, queries, keys, si
 
         def park_rows(j):
             bd = bds[j]
-            park = work.tile([P, PITCH], F32, tag="park", bufs=3)
-            nc.scalar.copy(out=park[:, 128:PITCH], in_=bd[:].rearrange("p t f -> p (t f)"))
-            nc.scalar.copy(out=park[:, 0:128], in_=bd[:, 1, 128:256])
-            parks[j] = park
+            if j % 2 == 0:
+                parks[j // 2] = work.tile([P, PITCH], F32, tag="park", bufs=3, name="park")
+            park = parks[j // 2]
+            col = 128 + 512 * (j % 2)
+            nc.scalar.copy(out=park[:, col : col + 512], in_=bd[:].rearrange("p t f -> p (t f)"))
+            if j % 2 == 1:
+                nc.scalar.copy(out=park[:, 0:128], in_=bd[:, 1, 128:256])
 
-        def park_write(j):
+        def park_write(m):
             nc.sync.dma_start(
-                out=o_flat[j, 0 : P * PITCH].rearrange("(p s) -> p s", s=PITCH), in_=parks[j][:]
+                out=o_flat[m, 0 : P * PITCH].rearrange("(p s) -> p s", s=PITCH), in_=parks[m][:]
             )
 
-        def read_back(j):
-            x = keep.tile([P, 4, 128], F32, tag="x", bufs=B_AHEAD + 2)
+        def read_back(m):
+            x = keep.tile([P, 8, 128], F32, tag="x", bufs=3)
             nc.sync.dma_start(
                 out=x[:].rearrange("p s j -> p (s j)"),
-                in_=o_flat[j, 128 : 128 + P * (PITCH - 1)].rearrange("(p s) -> p s", s=PITCH - 1)[:, 0:512],
+                in_=o_flat[m, 128 : 128 + P * (PITCH - 1)].rearrange("(p s) -> p s", s=PITCH - 1)[:, 0:1024],
             )
-            low = lows[j % (B_AHEAD + 2)]
-            for n in range(2):
-                shared = x[:, 2 * n, :]
+            low_a = lows[(2 * m) % 6]
+            low_b = lows[(2 * m + 1) % 6]
+            for shared, kept in ((0, low_b[:, 1, :]), (2, low_a[:, 2, :]), (4, low_a[:, 1, :]), (6, low_b[:, 2, :])):
                 nc.gpsimd.affine_select(
-                    out=low[:, 1 + n, :], in_=shared, pattern=[[-1, 128]],
+                    out=kept, in_=x[:, shared, :], pattern=[[-1, 128]],
                     compare_op=IS_GE, fill=0.0, base=-1, channel_multiplier=1,
                 )
                 nc.gpsimd.affine_select(
-                    out=shared, in_=shared, pattern=[[1, 128]],
+                    out=x[:, shared, :], in_=x[:, shared, :], pattern=[[1, 128]],
                     compare_op=IS_GE, fill=0.0, base=0, channel_multiplier=-1,
                 )
-            shifted[j] = (x, low)
+            shifted[2 * m] = (x[:, 0:4, :], low_a)
+            shifted[2 * m + 1] = (x[:, 4:8, :], low_b)
 
         def transpose_k(i, banks):
             words = k_raw[i][:].bitcast(F32)
@@ -251,7 +255,7 @@ def tile_gemma3naudiorelativepositionembedding_pa_t_kernel(tc, queries, keys, si
             x, low = shifted[i]
             a_seg = accs[(i, t)][:].rearrange("p (tt s r) -> p s r tt", tt=4, s=4)
             o_seg = res[:, t, :].rearrange("p (s r tt) -> p s r tt", s=4, tt=4)
-            x_seg = x[:].rearrange("p s (r tt) -> p s r tt", tt=4)
+            x_seg = x.rearrange("p s (r tt) -> p s r tt", tt=4)
             l_seg = low[:].rearrange("p s (r tt) -> p s r tt", tt=4)
             if t == 0:
                 nc.vector.tensor_tensor(out=o_seg[:, 0:2], in0=a_seg[:, 0:2], in1=x_seg[:, 0:2], op=ADD)
@@ -278,10 +282,10 @@ def tile_gemma3naudiorelativepositionembedding_pa_t_kernel(tc, queries, keys, si
             if 2 <= s + Q_LOAD < NBLK:
                 load_pair_rows(s + Q_LOAD, q_view[s + Q_LOAD])
             store_up_to(i_a - STORE_LAG if s + K_LOAD < NBLK else i_a - 1, nc.sync)
-            if 0 <= j_w < NBLK:
-                park_write(j_w)
-            if 0 <= j_r < NBLK:
-                read_back(j_r)
+            if 0 <= j_w < NBLK and j_w % 2 == 1:
+                park_write(j_w // 2)
+            if 0 <= j_r < NBLK and j_r % 2 == 1:
+                read_back(j_r // 2)
             if 0 <= j_t - 1 < NBLK:
                 quantise_q(j_t - 1)
             has_b = 0 <= j_b < NBLK
@@ -293,6 +297,8 @@ def tile_gemma3naudiorelativepositionembedding_pa_t_kernel(tc, queries, keys, si
                 positions(j_b, 0)
             if has_a:
                 add_up(i_a, 0)
+            if s == NBLK:
+                nc.sync.dma_start(out=o_view[i_a][:, 0, :], in_=results[i_a][:, 0, :])
             if has_k:
                 transpose_k(s, (3,))
             if j_t < NBLK:
@@ -308,4 +314,4 @@ def tile_gemma3naudiorelativepositionembedding_pa_t_kernel(tc, queries, keys, si
                 park_rows(j_b)
             if has_a:
                 add_up(i_a, 1)
-        store_up_to(NBLK - 1, nc.sync)
+        nc.sync.dma_start(out=o_view[NBLK - 1][:, 1, :], in_=results[NBLK - 1][:, 1, :])

@@ -19,10 +19,11 @@ D = 1024
 F = 256
 PITCH = 128 + 4 * F
 Q_AHEAD = 8
-B_AHEAD = 6
+B_AHEAD = 5
 K_LOAD = 2
 Q_LOAD = Q_AHEAD + 2
 STORE_LAG = 7
+FIRST_B = -4
 EARLY_K_LOADS = {-6: 0, -5: 1, -3: 2, -1: 3}
 
 FLOPS = 2 * F * D * D + NBLK * 2 * U * D * (C + F)
@@ -226,16 +227,19 @@ def tile_gemma3naudiorelativepositionembedding_pa_t_kernel(tc, queries, keys, si
         def quantise_k(i):
             k_codes = work.tile([P, 2 * C], U32, tag="k_codes", align_bytes=64)
             k_scales = work.tile([P, 2 * C], U8, tag="k_scales", align_bytes=64)
-            nc.vector.quantize_mx(out=k_codes[:].bitcast(FP8X4), scales=k_scales[:], in_=k_grouped[i][:])
+            for g in range(2):
+                nc.vector.quantize_mx(
+                    out=k_codes[:, 512 * g : 512 * g + 512].bitcast(FP8X4),
+                    scales=k_scales[:, 512 * g : 512 * g + 512],
+                    in_=k_grouped[i][:, 2048 * g : 2048 * g + 2048],
+                )
             k_mx[i] = (k_codes, k_scales)
 
         def content(i, t):
             q_codes, q_scales = q_mx[i]
             k_codes, k_scales = k_mx[i]
             acc = psum.tile([P, C], F32, tag="ac", bufs=2)
-            for g in (-1, 0, 1):
-                lone = g < 0
-                g = max(g, 0)
+            for g in range(2):
                 qcol = 256 * g + 128 * t
                 nc.tensor.matmul_mx(
                     out=acc[:],
@@ -244,7 +248,7 @@ def tile_gemma3naudiorelativepositionembedding_pa_t_kernel(tc, queries, keys, si
                     rhs=k_codes[:, 512 * g : 512 * g + 512].bitcast(FP8X4),
                     rhs_scale=k_scales[:, 512 * g : 512 * g + 512],
                     start=(g == 0),
-                    stop=(g == 1 or lone),
+                    stop=(g == 1),
                 )
             accs[(i, t)] = acc
 
@@ -272,7 +276,10 @@ def tile_gemma3naudiorelativepositionembedding_pa_t_kernel(tc, queries, keys, si
                 stored[0] += 1
 
         for s in range(-Q_AHEAD, NBLK + 1):
-            j_t, j_b, j_w, j_r, i_a = s + Q_AHEAD, s + B_AHEAD, s + B_AHEAD - 1, s + B_AHEAD - 2, s - 1
+            j_t, i_a = s + Q_AHEAD, s - 1
+            b_now = [j for j in range(NBLK) if max(j - B_AHEAD, FIRST_B) == s]
+            w_now = [m for m in range(NBLK // 2) if max(2 * m + 1 - B_AHEAD, FIRST_B) + 1 == s]
+            r_now = [m for m in range(NBLK // 2) if max(2 * m + 1 - B_AHEAD, FIRST_B) + 2 == s]
             has_k = 0 <= s < NBLK
             has_a = 0 <= i_a
             if s in EARLY_K_LOADS:
@@ -282,19 +289,21 @@ def tile_gemma3naudiorelativepositionembedding_pa_t_kernel(tc, queries, keys, si
             if 2 <= s + Q_LOAD < NBLK:
                 load_pair_rows(s + Q_LOAD, q_view[s + Q_LOAD])
             store_up_to(i_a - STORE_LAG if s + K_LOAD < NBLK else i_a - 1, nc.sync)
-            if 0 <= j_w < NBLK and j_w % 2 == 1:
-                park_write(j_w // 2)
-            if 0 <= j_r < NBLK and j_r % 2 == 1:
-                read_back(j_r // 2)
+            for m in w_now:
+                park_write(m)
+            for m in r_now:
+                read_back(m)
             if 0 <= j_t - 1 < NBLK:
                 quantise_q(j_t - 1)
-            has_b = 0 <= j_b < NBLK
             if has_k:
                 transpose_k(s, (0, 1, 2))
             if has_a:
                 content(i_a, 0)
-            if has_b:
-                positions(j_b, 0)
+            for j in b_now:
+                positions(j, 0)
+                if j != b_now[-1]:
+                    positions(j, 1)
+                    park_rows(j)
             if has_a:
                 add_up(i_a, 0)
             if s == NBLK:
@@ -309,9 +318,9 @@ def tile_gemma3naudiorelativepositionembedding_pa_t_kernel(tc, queries, keys, si
                 quantise_k(s)
             if has_a:
                 content(i_a, 1)
-            if has_b:
-                positions(j_b, 1)
-                park_rows(j_b)
+            for j in b_now[-1:]:
+                positions(j, 1)
+                park_rows(j)
             if has_a:
                 add_up(i_a, 1)
         nc.sync.dma_start(out=o_view[NBLK - 1][:, 1, :], in_=results[NBLK - 1][:, 1, :])

@@ -239,7 +239,9 @@ def tile_gemma3naudiorelativepositionembedding_pa_t_kernel(tc, queries, keys, si
             q_codes, q_scales = q_mx[i]
             k_codes, k_scales = k_mx[i]
             acc = psum.tile([P, C], F32, tag="ac", bufs=2)
-            for g in range(2):
+            for g in (-1, 0, 1) if i < NBLK - 1 else (0, 1):
+                lone = g < 0
+                g = max(g, 0)
                 qcol = 256 * g + 128 * t
                 nc.tensor.matmul_mx(
                     out=acc[:],
@@ -248,7 +250,7 @@ def tile_gemma3naudiorelativepositionembedding_pa_t_kernel(tc, queries, keys, si
                     rhs=k_codes[:, 512 * g : 512 * g + 512].bitcast(FP8X4),
                     rhs_scale=k_scales[:, 512 * g : 512 * g + 512],
                     start=(g == 0),
-                    stop=(g == 1),
+                    stop=(g == 1 or lone),
                 )
             accs[(i, t)] = acc
 

from contextlib import ExitStack

import concourse.mybir as mybir
from concourse.masks import make_identity

F32 = mybir.dt.float32
BF16 = mybir.dt.bfloat16
U32 = mybir.dt.uint32
U8 = mybir.dt.uint8
FP8X4 = mybir.dt.float8_e4m3fn_x4
ADD = mybir.AluOpType.add
IS_GE = mybir.AluOpType.is_ge

P = 128
NBLK = 16
U = 256
C = 512
D = 1024
F = 256
PITCH = 128 + 4 * F
Q_AHEAD = 8
B_AHEAD = 5
K_LOAD = 2
Q_LOAD = Q_AHEAD + 2
STORE_LAG = 7
FIRST_B = -4
EARLY_K_LOADS = {-6: 0, -5: 1, -3: 2, -1: 3}

FLOPS = 2 * F * D * D + NBLK * 2 * U * D * (C + F)


def tile_gemma3naudiorelativepositionembedding_pa_t_kernel(tc, queries, keys, sin_emb, pos_w, out):
    nc = tc.nc
    q_view = queries.rearrange("b w (p e) h d -> (b w) p (e h d)", e=2)
    k_view = keys.rearrange("b w (p t) h d -> (b w) p (t h d)", t=4)
    s_view = sin_emb.rearrange("(p e) i -> p (e i)", e=2)
    w_view = pos_w.rearrange("(h p e) i -> h p (e i)", h=4, e=2)
    o_view = out.rearrange("b h w (t p) c -> (b h w) p t c", t=2)
    o_flat = out.rearrange("b h (m w) u c -> (b h m) (w u c)", w=2)

    with ExitStack() as ctx:
        const = ctx.enter_context(tc.tile_pool(name="const", bufs=1))
        raws = ctx.enter_context(tc.tile_pool(name="raws", bufs=6))
        work = ctx.enter_context(tc.tile_pool(name="work", bufs=2))
        keep = ctx.enter_context(tc.tile_pool(name="keep", bufs=Q_AHEAD + 3))
        psum = ctx.enter_context(tc.psum_pool(name="psum", bufs=2))
        ctx.enter_context(tc.manual_schedule())

        pair_raw = {}
        k_raw = {}
        pair_grouped = {}
        q_mx = {}
        k_grouped = {}
        k_mx = {}
        accs = {}
        bds = {}
        parks = {}
        shifted = {}
        results = {}

        def load_pair_rows(key, src):
            raw = raws.tile([P, 2 * D], BF16, tag="qraw", bufs=8)
            nc.sync.dma_start(out=raw[:], in_=src)
            pair_raw[key] = raw

        def load_k(i):
            raw = raws.tile([P, 4 * D], BF16, tag="kraw", bufs=4)
            nc.sync.dma_start(out=raw[:], in_=k_view[i])
            k_raw[i] = raw

        load_pair_rows("s", s_view)
        for h in range(4):
            load_pair_rows("w%d" % h, w_view[h])
        for n in range(2):
            load_pair_rows(n, q_view[n])

        ident = const.tile([P, P], F32, name="ident")
        make_identity(nc, ident[:])
        lows = []
        for n in range(6):
            low = const.tile([P, 4, 128], F32, name="low%d" % n)
            nc.gpsimd.memset(low[:], 0.0)
            lows.append(low)

        def copy_out(engine, dst, src):
            if engine == 0:
                nc.scalar.copy(out=dst, in_=src)
            else:
                nc.vector.tensor_copy(out=dst, in_=src)

        def transpose_pair_rows(key, natural, engines):
            words = pair_raw[key][:].bitcast(F32)
            grouped = work.tile([P, 2 * U * 4], BF16, tag="qg", bufs=3, align_bytes=64)
            g32 = grouped[:].bitcast(F32).rearrange("p (g c u) -> p g c u", g=2, u=2)
            for g in range(2):
                bank = psum.tile([P, 4, P], F32, tag="tp", bufs=4)
                for e in range(2):
                    for u2 in range(2):
                        col = 512 * e + 128 * (2 * g + u2)
                        nc.tensor.transpose(bank[:, 2 * e + u2, :], words[:, col : col + 128], ident[:])
                if natural:
                    dst = g32[:, g].rearrange("p (r e) u -> p r e u", e=2)
                    bsrc = bank[:].rearrange("p (e u) r -> p r e u", e=2)
                else:
                    dst = g32[:, g].rearrange("p (e r) u -> p e r u", e=2)
                    bsrc = bank[:].rearrange("p (e u) r -> p e r u", e=2)
                copy_out(engines[g], dst, bsrc)
            pair_grouped[key] = grouped

        def quantise_pair_rows(key, codes, scales):
            nc.vector.quantize_mx(out=codes.bitcast(FP8X4), scales=scales, in_=pair_grouped[key][:])

        s_codes = const.tile([P, 2 * F], U32, name="s_codes", align_bytes=64)
        s_scales = const.tile([P, 2 * F], U8, name="s_scales", align_bytes=64)
        w_codes = const.tile([P, 4, 512], U32, name="w_codes", align_bytes=64)
        w_scales = const.tile([P, 4, 512], U8, name="w_scales", align_bytes=64)
        p_grouped = const.tile([P, 2 * F * 4], BF16, name="p_grouped", align_bytes=64)
        pg = p_grouped[:].rearrange("p (g f t) -> p g f t", g=2, t=4)
        p_codes = const.tile([P, 2 * F], U32, name="p_codes", align_bytes=64)
        p_scales = const.tile([P, 2 * F], U8, name="p_scales", align_bytes=64)

        transpose_pair_rows("s", True, (0, 1))
        transpose_pair_rows("w0", False, (0, 1))
        quantise_pair_rows("s", s_codes[:], s_scales[:])
        for h in range(1, 4):
            transpose_pair_rows("w%d" % h, False, (0, 1))
            quantise_pair_rows("w%d" % (h - 1), w_codes[:, h - 1, :], w_scales[:, h - 1, :])

        def project():
            quantise_pair_rows("w3", w_codes[:, 3, :], w_scales[:, 3, :])
            for g in range(2):
                for fh in range(2):
                    pb = psum.tile([P, 4, 128], F32, tag="bd", bufs=2)
                    for t in range(4):
                        h = 2 * g + t // 2
                        e = t % 2
                        for gi in range(2):
                            wcol = 256 * gi + 128 * e
                            scol = 256 * gi + 128 * fh
                            nc.tensor.matmul_mx(
                                out=pb[:, t, :],
                                lhsT=w_codes[:, h, wcol : wcol + 128].bitcast(FP8X4),
                                lhsT_scale=w_scales[:, h, wcol : wcol + 128],
                                rhs=s_codes[:, scol : scol + 128].bitcast(FP8X4),
                                rhs_scale=s_scales[:, scol : scol + 128],
                                start=(gi == 0),
                                stop=(gi == 1),
                            )
                    copy_out(fh, pg[:, g, 128 * fh : 128 * fh + 128, :], pb[:].rearrange("p t f -> p f t"))
            nc.vector.quantize_mx(out=p_codes[:].bitcast(FP8X4), scales=p_scales[:], in_=p_grouped[:])

        def quantise_q(j):
            q_codes = keep.tile([P, 2 * U], U32, tag="q_codes", align_bytes=64)
            q_scales = keep.tile([P, 2 * U], U8, tag="q_scales", align_bytes=64)
            quantise_pair_rows(j, q_codes[:], q_scales[:])
            q_mx[j] = (q_codes, q_scales)

        def positions(j, t):
            q_codes, q_scales = q_mx[j]
            if t == 0:
                bds[j] = psum.tile([P, 2, F], F32, tag="bd", bufs=2, name="bd")
            bd = bds[j]
            for g in range(2):
                qcol = 256 * g + 128 * t
                nc.tensor.matmul_mx(
                    out=bd[:, t, :],
                    lhsT=q_codes[:, qcol : qcol + 128].bitcast(FP8X4),
                    lhsT_scale=q_scales[:, qcol : qcol + 128],
                    rhs=p_codes[:, 256 * g : 256 * g + 256].bitcast(FP8X4),
                    rhs_scale=p_scales[:, 256 * g : 256 * g + 256],
                    start=(g == 0),
                    stop=(g == 1),
                )

        def park_rows(j):
            bd = bds[j]
            if j % 2 == 0:
                parks[j // 2] = work.tile([P, PITCH], F32, tag="park", bufs=3, name="park")
            park = parks[j // 2]
            col = 128 + 512 * (j % 2)
            nc.scalar.copy(out=park[:, col : col + 512], in_=bd[:].rearrange("p t f -> p (t f)"))
            if j % 2 == 1:
                nc.scalar.copy(out=park[:, 0:128], in_=bd[:, 1, 128:256])

        def park_write(m):
            nc.sync.dma_start(
                out=o_flat[m, 0 : P * PITCH].rearrange("(p s) -> p s", s=PITCH), in_=parks[m][:]
            )

        def read_back(m):
            x = keep.tile([P, 8, 128], F32, tag="x", bufs=3)
            nc.sync.dma_start(
                out=x[:].rearrange("p s j -> p (s j)"),
                in_=o_flat[m, 128 : 128 + P * (PITCH - 1)].rearrange("(p s) -> p s", s=PITCH - 1)[:, 0:1024],
            )
            low_a = lows[(2 * m) % 6]
            low_b = lows[(2 * m + 1) % 6]
            for shared, kept in ((0, low_b[:, 1, :]), (2, low_a[:, 2, :]), (4, low_a[:, 1, :]), (6, low_b[:, 2, :])):
                nc.gpsimd.affine_select(
                    out=kept, in_=x[:, shared, :], pattern=[[-1, 128]],
                    compare_op=IS_GE, fill=0.0, base=-1, channel_multiplier=1,
                )
                nc.gpsimd.affine_select(
                    out=x[:, shared, :], in_=x[:, shared, :], pattern=[[1, 128]],
                    compare_op=IS_GE, fill=0.0, base=0, channel_multiplier=-1,
                )
            shifted[2 * m] = (x[:, 0:4, :], low_a)
            shifted[2 * m + 1] = (x[:, 4:8, :], low_b)

        def transpose_k(i, banks):
            words = k_raw[i][:].bitcast(F32)
            if banks[0] == 0:
                k_grouped[i] = work.tile([P, 2 * C * 4], BF16, tag="kg", align_bytes=64, name="kg")
            grouped = k_grouped[i]
            g32 = grouped[:].bitcast(F32).rearrange("p (g n u) -> p g n u", g=2, u=2)
            for tt in banks:
                bank = psum.tile([P, 4, P], F32, tag="tp", bufs=4)
                for w in range(4):
                    col = 512 * tt + 128 * w
                    nc.tensor.transpose(bank[:, w, :], words[:, col : col + 128], ident[:])
                copy_out(
                    1 if tt == 3 else 0,
                    g32[:, :, 128 * tt : 128 * tt + 128, :],
                    bank[:].rearrange("p (g u) r -> p g r u", g=2),
                )

        def quantise_k(i):
            k_codes = work.tile([P, 2 * C], U32, tag="k_codes", align_bytes=64)
            k_scales = work.tile([P, 2 * C], U8, tag="k_scales", align_bytes=64)
            for g in range(2):
                nc.vector.quantize_mx(
                    out=k_codes[:, 512 * g : 512 * g + 512].bitcast(FP8X4),
                    scales=k_scales[:, 512 * g : 512 * g + 512],
                    in_=k_grouped[i][:, 2048 * g : 2048 * g + 2048],
                )
            k_mx[i] = (k_codes, k_scales)

        def content(i, t):
            q_codes, q_scales = q_mx[i]
            k_codes, k_scales = k_mx[i]
            acc = psum.tile([P, C], F32, tag="ac", bufs=2)
            for g in (-1, 0, 1) if i < NBLK - 1 else (0, 1):
                lone = g < 0
                g = max(g, 0)
                qcol = 256 * g + 128 * t
                nc.tensor.matmul_mx(
                    out=acc[:],
                    lhsT=q_codes[:, qcol : qcol + 128].bitcast(FP8X4),
                    lhsT_scale=q_scales[:, qcol : qcol + 128],
                    rhs=k_codes[:, 512 * g : 512 * g + 512].bitcast(FP8X4),
                    rhs_scale=k_scales[:, 512 * g : 512 * g + 512],
                    start=(g == 0),
                    stop=(g == 1 or lone),
                )
            accs[(i, t)] = acc

        def add_up(i, t):
            if t == 0:
                results[i] = work.tile([P, 2, C], F32, tag="res", bufs=STORE_LAG + 2, name="res")
            res = results[i]
            x, low = shifted[i]
            a_seg = accs[(i, t)][:].rearrange("p (tt s r) -> p s r tt", tt=4, s=4)
            o_seg = res[:, t, :].rearrange("p (s r tt) -> p s r tt", s=4, tt=4)
            x_seg = x.rearrange("p s (r tt) -> p s r tt", tt=4)
            l_seg = low[:].rearrange("p s (r tt) -> p s r tt", tt=4)
            if t == 0:
                nc.vector.tensor_tensor(out=o_seg[:, 0:2], in0=a_seg[:, 0:2], in1=x_seg[:, 0:2], op=ADD)
                nc.vector.tensor_tensor(out=o_seg[:, 2:4], in0=a_seg[:, 2:4], in1=l_seg[:, 2:4], op=ADD)
            else:
                nc.vector.tensor_tensor(out=o_seg[:, 1:3], in0=a_seg[:, 1:3], in1=x_seg[:, 2:4], op=ADD)
                nc.vector.tensor_tensor(out=o_seg[:, 0:4:3], in0=a_seg[:, 0:4:3], in1=l_seg[:, 0:2], op=ADD)

        stored = [0]

        def store_up_to(last, queue):
            while stored[0] <= last:
                queue.dma_start(out=o_view[stored[0]], in_=results[stored[0]][:])
                stored[0] += 1

        for s in range(-Q_AHEAD, NBLK + 1):
            j_t, i_a = s + Q_AHEAD, s - 1
            b_now = [j for j in range(NBLK) if max(j - B_AHEAD, FIRST_B) == s]
            w_now = [m for m in range(NBLK // 2) if max(2 * m + 1 - B_AHEAD, FIRST_B) + 1 == s]
            r_now = [m for m in range(NBLK // 2) if max(2 * m + 1 - B_AHEAD, FIRST_B) + 2 == s]
            has_k = 0 <= s < NBLK
            has_a = 0 <= i_a
            if s in EARLY_K_LOADS:
                load_k(EARLY_K_LOADS[s])
            elif 4 <= s + K_LOAD < NBLK:
                load_k(s + K_LOAD)
            if 2 <= s + Q_LOAD < NBLK:
                load_pair_rows(s + Q_LOAD, q_view[s + Q_LOAD])
            store_up_to(i_a - STORE_LAG if s + K_LOAD < NBLK else i_a - 1, nc.sync)
            for m in w_now:
                park_write(m)
            for m in r_now:
                read_back(m)
            if 0 <= j_t - 1 < NBLK:
                quantise_q(j_t - 1)
            if has_k:
                transpose_k(s, (0, 1, 2))
            if has_a:
                content(i_a, 0)
            for j in b_now:
                positions(j, 0)
                if j != b_now[-1]:
                    positions(j, 1)
                    park_rows(j)
            if has_a:
                add_up(i_a, 0)
            if s == NBLK:
                nc.sync.dma_start(out=o_view[i_a][:, 0, :], in_=results[i_a][:, 0, :])
            if has_k:
                transpose_k(s, (3,))
            if j_t < NBLK:
                transpose_pair_rows(j_t, True, (0, 0))
            if s == -Q_AHEAD:
                project()
            if has_k:
                quantise_k(s)
            if has_a:
                content(i_a, 1)
            for j in b_now[-1:]:
                positions(j, 1)
                park_rows(j)
            if has_a:
                add_up(i_a, 1)
        nc.sync.dma_start(out=o_view[NBLK - 1][:, 1, :], in_=results[NBLK - 1][:, 1, :])
